import numpy as np
import ml_dtypes


def mxq(x, axis, fmt="e4m3"):
    dtype, down = {"e4m3": (ml_dtypes.float8_e4m3fn, 7), "e5m2": (ml_dtypes.float8_e5m2, 14)}[fmt]
    v = np.moveaxis(np.asarray(x, np.float32).astype(ml_dtypes.bfloat16).astype(np.float64), axis, -1)
    blocks = v.reshape(v.shape[:-1] + (-1, 32))
    amax = np.abs(blocks).max(-1, keepdims=True)
    byte = np.maximum(np.where(amax > 0, np.frexp(amax)[1] - 1 + 127, 0) - down, 1)
    scale = np.exp2(byte - 127.0)
    codes = (blocks / scale).astype(np.float32).astype(dtype).astype(np.float64)
    return np.moveaxis((codes * scale).reshape(v.shape), -1, axis)


WIDE = False


def mx_kscale(k):
    if not WIDE:
        return np.ones(k)
    levels = np.array([10, -10, 5, -5, 0])
    a = np.random.permutation(np.resize(levels, k // 512 * 4)).reshape(k // 512, 4)
    idx = np.arange(k)
    return np.exp2(a[idx // 512, idx % 128 // 32])


BF16 = ml_dtypes.bfloat16


def bf(x):
    return np.asarray(x, np.float32).astype(BF16)


def f64(x):
    return np.asarray(x).astype(np.float64)


B, N, D = 1, 1024, 512


def setup_inputs():
    s = mx_kscale(D)
    m = np.random.uniform(0.25, 1.75, (B, N, 1))
    return {"q": bf(np.random.standard_normal((B, N, D)) * 3.0 * m),
            "k": bf(np.random.standard_normal((B, N, D)) * 3.0 * m),
            "x": bf(np.random.standard_normal((B, N, D)) * m * s),
            "Wv": bf(np.random.standard_normal((D, D)) * 3.0 / np.sqrt(D) / s[None, :])}


def reference(q, k, x, Wv):
    q, k = f64(q), f64(k)
    v = mxq(f64(x), 2, "e4m3") @ mxq(f64(Wv), 1, "e4m3").T
    qk = mxq(q, 2, "e4m3") @ mxq(k, 2, "e4m3").transpose(0, 2, 1)
    d2 = (q * q).sum(-1)[:, :, None] + (k * k).sum(-1)[:, None, :] - 2.0 * qk
    sc = np.sqrt(np.maximum(d2, 0.0)) / np.sqrt(D)
    e = np.exp(sc - sc.max(-1, keepdims=True))
    return (mxq(e, 2, "e4m3") @ mxq(v, 1, "e4m3")) / e.sum(-1, keepdims=True)

@@ -1,0 +1,294 @@
+from contextlib import ExitStack
+
+import concourse.mybir as mybir
+from concourse.masks import make_identity
+
+F32 = mybir.dt.float32
+BF16 = mybir.dt.bfloat16
+U32 = mybir.dt.uint32
+U8 = mybir.dt.uint8
+FP8X4 = mybir.dt.float8_e4m3fn_x4
+ALU = mybir.AluOpType
+ACT = mybir.ActivationFunctionType
+
+P = 128
+PACK = 4
+K_PASS = P * PACK
+TOKENS = 1024
+FEATS = 512
+TILES = TOKENS // P
+CHUNKS = TOKENS // K_PASS
+HALVES = FEATS // 2 // P
+ROW = TOKENS + 8
+FINISH_LAG = 4
+
+FLOPS = 2 * TOKENS * FEATS * FEATS + 2 * 2 * TOKENS * TOKENS * FEATS
+
+
+def load_tokens(nc, pool, src, name):
+    rows = pool.tile([P, CHUNKS, PACK, FEATS], BF16, name=name)
+    view = src.flatten_outer_dims().rearrange("(c p t) f -> p c t f", p=P, t=PACK)
+    for c in range(CHUNKS):
+        nc.sync.dma_start(out=rows[:, c], in_=view[:, c])
+    return rows
+
+
+def mx_tiles(pool, width, name):
+    grouped = pool.tile([P, width, PACK], BF16, name=name + "_grouped", align_bytes=64)
+    codes = pool.tile([P, width], U32, name=name + "_codes", align_bytes=64)
+    scales = pool.tile([P, width], U8, name=name + "_scales", align_bytes=64)
+    return grouped, codes, scales
+
+
+def quantise(nc, operand, cols):
+    grouped, codes, scales = operand
+    nc.vector.quantize_mx(
+        out=codes[:, cols].bitcast(FP8X4),
+        scales=scales[:, cols],
+        in_=grouped[:, cols, :].rearrange("p m t -> p (m t)"),
+    )
+
+
+def multiply(nc, acc, stationary, s_cols, moving, m_cols, start, stop):
+    nc.tensor.matmul_mx(
+        out=acc,
+        lhsT=stationary[1][:, s_cols].bitcast(FP8X4),
+        lhsT_scale=stationary[2][:, s_cols],
+        rhs=moving[1][:, m_cols].bitcast(FP8X4),
+        rhs_scale=moving[2][:, m_cols],
+        start=start,
+        stop=stop,
+    )
+
+
+def block(index, size):
+    return slice(index * size, (index + 1) * size)
+
+
+def tile_attention_pa_kernel(tc, q, k, x, Wv, out):
+    nc = tc.nc
+    with ExitStack() as ctx:
+        ctx.enter_context(tc.manual_schedule())
+        keep = ctx.enter_context(tc.tile_pool(name="keep", bufs=1))
+        work = ctx.enter_context(tc.tile_pool(name="work", bufs=3))
+        results = ctx.enter_context(tc.tile_pool(name="results", bufs=4))
+        psum = ctx.enter_context(tc.psum_pool(name="psum", bufs=4))
+
+        k_rows = load_tokens(nc, keep, k, "k_rows")
+        q_rows = load_tokens(nc, keep, q, "q_rows")
+        w_rows = keep.tile([P, 1, FEATS // P, FEATS], BF16, name="w_rows")
+        nc.sync.dma_start(out=w_rows[:, 0], in_=Wv.rearrange("(r p) f -> p r f", p=P))
+        x_rows = load_tokens(nc, keep, x, "x_rows")
+
+        ident_f32 = keep.tile([P, P], F32, name="ident_f32")
+        make_identity(nc, ident_f32[:])
+        ident_bf16 = keep.tile([P, P], BF16, name="ident_bf16")
+        make_identity(nc, ident_bf16[:])
+
+        one = keep.tile([P, 1], F32, name="one")
+        nc.vector.memset(one[:], 1.0)
+        warm = keep.tile([P, 1], F32, name="warm")
+        nc.scalar.activation(out=warm[:], in_=one[:], func=ACT.Sqrt)
+
+        k_mx = mx_tiles(keep, TOKENS, "k")
+        q_mx = mx_tiles(keep, TOKENS, "q")
+        x_mx = mx_tiles(keep, TOKENS, "x")
+        w_mx = mx_tiles(keep, FEATS, "w")
+        v_mx = mx_tiles(keep, CHUNKS * FEATS, "v")
+
+        k_sq = keep.tile([P, TILES], F32, name="k_sq")
+        q_sq = keep.tile([P, TILES], F32, name="q_sq")
+        q_sq_half = keep.tile([P, TILES], F32, name="q_sq_half")
+        k_sq_half = keep.tile([P, TOKENS], F32, name="k_sq_half")
+        scores = keep.tile([P, TILES, ROW], F32, name="scores")
+        neg_max = keep.tile([P, TILES], F32, name="neg_max")
+        row_sum = keep.tile([P, TILES], F32, name="row_sum")
+        row_inv = keep.tile([P, TILES], F32, name="row_inv")
+        out_view = out.flatten_outer_dims().rearrange("(c p t) d -> p c t d", p=P, t=PACK)
+
+        def sum_of_squares(rows, sums, g):
+            squares = work.tile([P, FEATS], BF16, tag="squares")
+            nc.scalar.activation(
+                out=squares[:],
+                in_=rows[:, g // PACK, g % PACK, :],
+                func=ACT.Square,
+                accum_out=sums[:, g : g + 1],
+            )
+
+        def features_to_partitions(rows, operand, c, copy):
+            words = rows[:].bitcast(F32)
+            grouped_words = operand[0][:].bitcast(F32)
+            for pair in range(PACK // 2):
+                bank = psum.tile([P, HALVES, 2 * P], F32, tag="tp")
+                for a in range(2):
+                    for u in range(HALVES):
+                        nc.tensor.transpose(
+                            bank[:, u, block(a, P)], words[:, c, 2 * pair + a, block(u, P)], ident_f32[:]
+                        )
+                copy(
+                    out=grouped_words[:, block(2 * c + pair, 2 * P), :],
+                    in_=bank[:].rearrange("p u m -> p m u"),
+                )
+
+        def spread_key_squares(c):
+            bank = psum.tile([P, PACK, P], F32, tag="tp")
+            for t in range(PACK):
+                g = c * PACK + t
+                nc.tensor.transpose(
+                    bank[:, t, :], k_sq[:, g : g + 1].to_broadcast([P, P]), ident_f32[:]
+                )
+            return bank[:].rearrange("p t m -> p (t m)")
+
+        for g in range(PACK):
+            sum_of_squares(k_rows, k_sq, g)
+        features_to_partitions(k_rows, k_mx, 0, nc.vector.tensor_copy)
+        for g in range(PACK, TILES):
+            sum_of_squares(k_rows, k_sq, g)
+        features_to_partitions(k_rows, k_mx, 1, nc.vector.tensor_copy)
+        quantise(nc, k_mx, block(0, K_PASS))
+        spread_0 = spread_key_squares(0)
+
+        def query_squares(g):
+            sum_of_squares(q_rows, q_sq, g)
+            nc.gpsimd.tensor_scalar(
+                out=q_sq_half[:, g : g + 1],
+                in0=q_sq[:, g : g + 1],
+                scalar1=0.5,
+                scalar2=0.0,
+                op0=ALU.mult,
+                op1=ALU.add,
+            )
+
+        query_squares(0)
+        features_to_partitions(q_rows, q_mx, 0, nc.vector.tensor_copy)
+        quantise(nc, k_mx, block(1, K_PASS))
+        quantise(nc, q_mx, block(0, K_PASS))
+        nc.vector.tensor_scalar_mul(out=k_sq_half[:, block(0, K_PASS)], in0=spread_0, scalar1=0.5)
+        nc.scalar.mul(out=k_sq_half[:, block(1, K_PASS)], in_=spread_key_squares(1), mul=0.5)
+        query_squares(1)
+
+        def products(g):
+            banks = []
+            for c in range(CHUNKS):
+                qk = psum.tile([P, K_PASS], F32, tag="mm")
+                multiply(nc, qk[:], q_mx, block(g, P), k_mx, block(c, K_PASS), True, True)
+                banks.append(qk)
+            return banks
+
+        def distances(g, banks):
+            for c in range(CHUNKS):
+                nc.vector.scalar_tensor_tensor(
+                    out=scores[:, g, block(c, K_PASS)],
+                    in0=banks[c][:],
+                    scalar=q_sq_half[:, g : g + 1],
+                    in1=k_sq_half[:, block(c, K_PASS)],
+                    op0=ALU.subtract,
+                    op1=ALU.subtract,
+                )
+            nc.vector.tensor_scalar(
+                out=scores[:, g, 0:TOKENS],
+                in0=scores[:, g, 0:TOKENS],
+                scalar1=0.0,
+                scalar2=None,
+                op0=ALU.min,
+                op1=ALU.min,
+                accum_out=scores[:, g, TOKENS : TOKENS + 1],
+            )
+
+        def roots(g):
+            nc.scalar.activation(
+                out=scores[:, g, 0 : TOKENS + 1],
+                in_=scores[:, g, 0 : TOKENS + 1],
+                func=ACT.Sqrt,
+                scale=-2.0 / FEATS,
+            )
+            nc.gpsimd.tensor_scalar(
+                out=neg_max[:, g : g + 1],
+                in0=scores[:, g, TOKENS : TOKENS + 1],
+                scalar1=-1.0,
+                scalar2=0.0,
+                op0=ALU.mult,
+                op1=ALU.add,
+            )
+
+        def value_block(c, r, copy):
+            bank = psum.tile([P, PACK, P], F32, tag="tp")
+            for t in range(PACK):
+                multiply(nc, bank[:, t, :], x_mx, block(c * PACK + t, P), w_mx, block(r, P), True, True)
+            copy(
+                out=v_mx[0][:, block(c * PACK + r, P), :], in_=bank[:].rearrange("p t d -> p d t")
+            )
+
+        late = ((q_rows, q_mx, 1), (w_rows, w_mx, 0), (x_rows, x_mx, 0), (x_rows, x_mx, 1))
+        banks = products(0)
+        for g in range(TILES):
+            next_banks = products(g + 1) if g + 1 < TILES else None
+            if g + 2 < TILES:
+                query_squares(g + 2)
+            if g < len(late):
+                rows, operand, c = late[g]
+                features_to_partitions(rows, operand, c, nc.scalar.copy)
+            else:
+                value_block(0, g - len(late), nc.scalar.copy)
+            distances(g, banks)
+            if g < len(late) - 1:
+                quantise(nc, operand, block(c, K_PASS))
+            roots(g)
+            banks = next_banks
+
+        quantise(nc, x_mx, block(1, K_PASS))
+        quantise(nc, v_mx, block(0, FEATS))
+        for r in range(PACK):
+            value_block(1, r, nc.vector.tensor_copy)
+        quantise(nc, v_mx, block(1, FEATS))
+
+        def weights(g):
+            e_rows = work.tile([P, TOKENS], BF16, tag="e_rows")
+            nc.scalar.activation(
+                out=e_rows[:],
+                in_=scores[:, g, 0:TOKENS],
+                func=ACT.Exp,
+                bias=neg_max[:, g : g + 1],
+                scale=1.0,
+                accum_out=row_sum[:, g : g + 1],
+            )
+            bank = psum.tile([P, TILES, P], BF16, tag="tp")
+            for j in range(TILES):
+                nc.tensor.transpose(bank[:, j, :], e_rows[:, block(j, P)], ident_bf16[:])
+            e_grouped = work.tile([P, CHUNKS * P, PACK], BF16, tag="e_grouped", align_bytes=64)
+            e_codes = work.tile([P, CHUNKS * P], U32, tag="e_codes", align_bytes=64)
+            e_scales = work.tile([P, CHUNKS * P], U8, tag="e_scales", align_bytes=64)
+            if g % PACK == PACK - 1:
+                nc.vector.reciprocal(
+                    out=row_inv[:, g + 1 - PACK : g + 1], in_=row_sum[:, g + 1 - PACK : g + 1]
+                )
+            nc.vector.tensor_copy(
+                out=e_grouped[:].rearrange("p (c i) t -> p c i t", c=CHUNKS),
+                in_=bank[:].rearrange("p (c t) i -> p c i t", c=CHUNKS),
+            )
+            e_mx = (e_grouped, e_codes, e_scales)
+            quantise(nc, e_mx, block(0, CHUNKS * P))
+            return e_mx
+
+        def weighted_sum(e_mx):
+            acc = psum.tile([P, FEATS], F32, tag="mm")
+            for c in range(CHUNKS):
+                multiply(nc, acc[:], e_mx, block(c, P), v_mx, block(c, FEATS), c == 0, c == CHUNKS - 1)
+            return acc
+
+        def finish(g, acc):
+            result = results.tile([P, FEATS], F32, tag="result")
+            nc.scalar.activation(
+                out=result[:], in_=acc[:], func=ACT.Copy, scale=row_inv[:, g : g + 1]
+            )
+            nc.sync.dma_start(out=out_view[:, g // PACK, g % PACK, :], in_=result[:])
+
+        e_of = {}
+        acc_of = {}
+        for step in range(TILES + FINISH_LAG):
+            if step < TILES:
+                e_of[step] = weights(step)
+            if 1 <= step <= TILES:
+                acc_of[step - 1] = weighted_sum(e_of[step - 1])
+            if step >= FINISH_LAG:
+                finish(step - FINISH_LAG, acc_of[step - FINISH_LAG])

@@ -20,7 +20,9 @@ TILES = TOKENS // P
 CHUNKS = TOKENS // K_PASS
 HALVES = FEATS // 2 // P
 ROW = TOKENS + 8
-FINISH_LAG = 4
+QUANTISE_LAG = 1
+MULTIPLY_LAG = 2
+FINISH_LAG = 5
 
 FLOPS = 2 * TOKENS * FEATS * FEATS + 2 * 2 * TOKENS * TOKENS * FEATS
 
@@ -166,6 +168,7 @@ def tile_attention_pa_kernel(tc, q, k, x, Wv, out):
         nc.vector.tensor_scalar_mul(out=k_sq_half[:, block(0, K_PASS)], in0=spread_0, scalar1=0.5)
         nc.scalar.mul(out=k_sq_half[:, block(1, K_PASS)], in_=spread_key_squares(1), mul=0.5)
         query_squares(1)
+        query_squares(2)
 
         def products(g):
             banks = []
@@ -175,16 +178,17 @@ def tile_attention_pa_kernel(tc, q, k, x, Wv, out):
                 banks.append(qk)
             return banks
 
-        def distances(g, banks):
-            for c in range(CHUNKS):
-                nc.vector.scalar_tensor_tensor(
-                    out=scores[:, g, block(c, K_PASS)],
-                    in0=banks[c][:],
-                    scalar=q_sq_half[:, g : g + 1],
-                    in1=k_sq_half[:, block(c, K_PASS)],
-                    op0=ALU.subtract,
-                    op1=ALU.subtract,
-                )
+        def subtract(g, c, bank):
+            nc.vector.scalar_tensor_tensor(
+                out=scores[:, g, block(c, K_PASS)],
+                in0=bank[:],
+                scalar=q_sq_half[:, g : g + 1],
+                in1=k_sq_half[:, block(c, K_PASS)],
+                op0=ALU.subtract,
+                op1=ALU.subtract,
+            )
+
+        def clamp(g):
             nc.vector.tensor_scalar(
                 out=scores[:, g, 0:TOKENS],
                 in0=scores[:, g, 0:TOKENS],
@@ -220,27 +224,32 @@ def tile_attention_pa_kernel(tc, q, k, x, Wv, out):
             )
 
         late = ((q_rows, q_mx, 1), (w_rows, w_mx, 0), (x_rows, x_mx, 0), (x_rows, x_mx, 1))
-        banks = products(0)
+        banks = {0: products(0), 1: products(1)}
+        subtract(0, 0, banks[0][0])
+        subtract(0, 1, banks[0][1])
         for g in range(TILES):
-            next_banks = products(g + 1) if g + 1 < TILES else None
-            if g + 2 < TILES:
-                query_squares(g + 2)
+            if g + 3 < TILES:
+                query_squares(g + 3)
             if g < len(late):
                 rows, operand, c = late[g]
                 features_to_partitions(rows, operand, c, nc.scalar.copy)
             else:
                 value_block(0, g - len(late), nc.scalar.copy)
-            distances(g, banks)
+            if g + 2 < TILES:
+                banks[g + 2] = products(g + 2)
+            if g + 1 < TILES:
+                subtract(g + 1, 0, banks[g + 1][0])
+            clamp(g)
+            if g + 1 < TILES:
+                subtract(g + 1, 1, banks[g + 1][1])
             if g < len(late) - 1:
                 quantise(nc, operand, block(c, K_PASS))
             roots(g)
-            banks = next_banks
 
         quantise(nc, x_mx, block(1, K_PASS))
         quantise(nc, v_mx, block(0, FEATS))
         for r in range(PACK):
             value_block(1, r, nc.vector.tensor_copy)
-        quantise(nc, v_mx, block(1, FEATS))
 
         def weights(g):
             e_rows = work.tile([P, TOKENS], BF16, tag="e_rows")
@@ -256,8 +265,6 @@ def tile_attention_pa_kernel(tc, q, k, x, Wv, out):
             for j in range(TILES):
                 nc.tensor.transpose(bank[:, j, :], e_rows[:, block(j, P)], ident_bf16[:])
             e_grouped = work.tile([P, CHUNKS * P, PACK], BF16, tag="e_grouped", align_bytes=64)
-            e_codes = work.tile([P, CHUNKS * P], U32, tag="e_codes", align_bytes=64)
-            e_scales = work.tile([P, CHUNKS * P], U8, tag="e_scales", align_bytes=64)
             if g % PACK == PACK - 1:
                 nc.vector.reciprocal(
                     out=row_inv[:, g + 1 - PACK : g + 1], in_=row_sum[:, g + 1 - PACK : g + 1]
@@ -266,6 +273,11 @@ def tile_attention_pa_kernel(tc, q, k, x, Wv, out):
                 out=e_grouped[:].rearrange("p (c i) t -> p c i t", c=CHUNKS),
                 in_=bank[:].rearrange("p (c t) i -> p c i t", c=CHUNKS),
             )
+            return e_grouped
+
+        def quantise_weights(e_grouped):
+            e_codes = work.tile([P, CHUNKS * P], U32, tag="e_codes", align_bytes=64)
+            e_scales = work.tile([P, CHUNKS * P], U8, tag="e_scales", align_bytes=64)
             e_mx = (e_grouped, e_codes, e_scales)
             quantise(nc, e_mx, block(0, CHUNKS * P))
             return e_mx
@@ -283,12 +295,17 @@ def tile_attention_pa_kernel(tc, q, k, x, Wv, out):
             )
             nc.sync.dma_start(out=out_view[:, g // PACK, g % PACK, :], in_=result[:])
 
+        grouped_of = {}
         e_of = {}
         acc_of = {}
         for step in range(TILES + FINISH_LAG):
             if step < TILES:
-                e_of[step] = weights(step)
-            if 1 <= step <= TILES:
-                acc_of[step - 1] = weighted_sum(e_of[step - 1])
+                grouped_of[step] = weights(step)
+            if step == 0:
+                quantise(nc, v_mx, block(1, FEATS))
+            if 0 <= step - QUANTISE_LAG < TILES:
+                e_of[step - QUANTISE_LAG] = quantise_weights(grouped_of[step - QUANTISE_LAG])
+            if 0 <= step - MULTIPLY_LAG < TILES:
+                acc_of[step - MULTIPLY_LAG] = weighted_sum(e_of[step - MULTIPLY_LAG])
             if step >= FINISH_LAG:
                 finish(step - FINISH_LAG, acc_of[step - FINISH_LAG])

@@ -70,7 +70,6 @@ def block(index, size):
 def tile_attention_pa_kernel(tc, q, k, x, Wv, out):
     nc = tc.nc
     with ExitStack() as ctx:
-        ctx.enter_context(tc.manual_schedule())
         keep = ctx.enter_context(tc.tile_pool(name="keep", bufs=1))
         work = ctx.enter_context(tc.tile_pool(name="work", bufs=3))
         results = ctx.enter_context(tc.tile_pool(name="results", bufs=4))

@@ -18,8 +18,10 @@ TOKENS = 1024
 FEATS = 512
 TILES = TOKENS // P
 CHUNKS = TOKENS // K_PASS
+BOTH = (0, 1)
 HALVES = FEATS // 2 // P
 ROW = TOKENS + 8
+
 QUANTISE_LAG = 1
 MULTIPLY_LAG = 2
 FINISH_LAG = 5
@@ -27,11 +29,17 @@ FINISH_LAG = 5
 FLOPS = 2 * TOKENS * FEATS * FEATS + 2 * 2 * TOKENS * TOKENS * FEATS
 
 
-def load_tokens(nc, pool, src, name):
+def part(index, size):
+    return slice(index * size, (index + 1) * size)
+
+
+def load_tokens(nc, pool, src, name, tiles_a_load):
     rows = pool.tile([P, CHUNKS, PACK, FEATS], BF16, name=name)
     view = src.flatten_outer_dims().rearrange("(c p t) f -> p c t f", p=P, t=PACK)
     for c in range(CHUNKS):
-        nc.sync.dma_start(out=rows[:, c], in_=view[:, c])
+        for i in range(PACK // tiles_a_load):
+            tiles = part(i, tiles_a_load)
+            nc.sync.dma_start(out=rows[:, c, tiles], in_=view[:, c, tiles])
     return rows
 
 
@@ -63,23 +71,20 @@ def multiply(nc, acc, stationary, s_cols, moving, m_cols, start, stop):
     )
 
 
-def block(index, size):
-    return slice(index * size, (index + 1) * size)
-
-
 def tile_attention_pa_kernel(tc, q, k, x, Wv, out):
     nc = tc.nc
     with ExitStack() as ctx:
+        ctx.enter_context(tc.manual_schedule())
         keep = ctx.enter_context(tc.tile_pool(name="keep", bufs=1))
         work = ctx.enter_context(tc.tile_pool(name="work", bufs=3))
         results = ctx.enter_context(tc.tile_pool(name="results", bufs=4))
         psum = ctx.enter_context(tc.psum_pool(name="psum", bufs=4))
 
-        k_rows = load_tokens(nc, keep, k, "k_rows")
-        q_rows = load_tokens(nc, keep, q, "q_rows")
+        k_rows = load_tokens(nc, keep, k, "k_rows", 2)
+        q_rows = load_tokens(nc, keep, q, "q_rows", PACK)
         w_rows = keep.tile([P, 1, FEATS // P, FEATS], BF16, name="w_rows")
         nc.sync.dma_start(out=w_rows[:, 0], in_=Wv.rearrange("(r p) f -> p r f", p=P))
-        x_rows = load_tokens(nc, keep, x, "x_rows")
+        x_rows = load_tokens(nc, keep, x, "x_rows", PACK)
 
         ident_f32 = keep.tile([P, P], F32, name="ident_f32")
         make_identity(nc, ident_f32[:])
@@ -116,18 +121,18 @@ def tile_attention_pa_kernel(tc, q, k, x, Wv, out):
                 accum_out=sums[:, g : g + 1],
             )
 
-        def features_to_partitions(rows, operand, c, copy):
+        def features_to_partitions(rows, operand, c, pairs, copy):
             words = rows[:].bitcast(F32)
             grouped_words = operand[0][:].bitcast(F32)
-            for pair in range(PACK // 2):
+            for pair in pairs:
                 bank = psum.tile([P, HALVES, 2 * P], F32, tag="tp")
                 for a in range(2):
                     for u in range(HALVES):
                         nc.tensor.transpose(
-                            bank[:, u, block(a, P)], words[:, c, 2 * pair + a, block(u, P)], ident_f32[:]
+                            bank[:, u, part(a, P)], words[:, c, 2 * pair + a, part(u, P)], ident_f32[:]
                         )
                 copy(
-                    out=grouped_words[:, block(2 * c + pair, 2 * P), :],
+                    out=grouped_words[:, part(2 * c + pair, 2 * P), :],
                     in_=bank[:].rearrange("p u m -> p m u"),
                 )
 
@@ -140,15 +145,6 @@ def tile_attention_pa_kernel(tc, q, k, x, Wv, out):
                 )
             return bank[:].rearrange("p t m -> p (t m)")
 
-        for g in range(PACK):
-            sum_of_squares(k_rows, k_sq, g)
-        features_to_partitions(k_rows, k_mx, 0, nc.vector.tensor_copy)
-        for g in range(PACK, TILES):
-            sum_of_squares(k_rows, k_sq, g)
-        features_to_partitions(k_rows, k_mx, 1, nc.vector.tensor_copy)
-        quantise(nc, k_mx, block(0, K_PASS))
-        spread_0 = spread_key_squares(0)
-
         def query_squares(g):
             sum_of_squares(q_rows, q_sq, g)
             nc.gpsimd.tensor_scalar(
@@ -160,29 +156,38 @@ def tile_attention_pa_kernel(tc, q, k, x, Wv, out):
                 op1=ALU.add,
             )
 
+        for g in range(PACK):
+            sum_of_squares(k_rows, k_sq, g)
+        features_to_partitions(k_rows, k_mx, 0, BOTH, nc.vector.tensor_copy)
+        for g in range(PACK, TILES):
+            sum_of_squares(k_rows, k_sq, g)
+        features_to_partitions(k_rows, k_mx, 1, BOTH, nc.vector.tensor_copy)
+        quantise(nc, k_mx, part(0, K_PASS))
+        spread_0 = spread_key_squares(0)
         query_squares(0)
-        features_to_partitions(q_rows, q_mx, 0, nc.vector.tensor_copy)
-        quantise(nc, k_mx, block(1, K_PASS))
-        quantise(nc, q_mx, block(0, K_PASS))
-        nc.vector.tensor_scalar_mul(out=k_sq_half[:, block(0, K_PASS)], in0=spread_0, scalar1=0.5)
-        nc.scalar.mul(out=k_sq_half[:, block(1, K_PASS)], in_=spread_key_squares(1), mul=0.5)
+        features_to_partitions(q_rows, q_mx, 0, (0,), nc.vector.tensor_copy)
+        quantise(nc, k_mx, part(1, K_PASS))
+        quantise(nc, q_mx, part(0, 2 * P))
+        nc.vector.tensor_scalar_mul(out=k_sq_half[:, part(0, K_PASS)], in0=spread_0, scalar1=0.5)
+        nc.scalar.mul(out=k_sq_half[:, part(1, K_PASS)], in_=spread_key_squares(1), mul=0.5)
         query_squares(1)
+        features_to_partitions(q_rows, q_mx, 0, (1,), nc.scalar.copy)
         query_squares(2)
 
         def products(g):
             banks = []
             for c in range(CHUNKS):
                 qk = psum.tile([P, K_PASS], F32, tag="mm")
-                multiply(nc, qk[:], q_mx, block(g, P), k_mx, block(c, K_PASS), True, True)
+                multiply(nc, qk[:], q_mx, part(g, P), k_mx, part(c, K_PASS), True, True)
                 banks.append(qk)
             return banks
 
         def subtract(g, c, bank):
             nc.vector.scalar_tensor_tensor(
-                out=scores[:, g, block(c, K_PASS)],
+                out=scores[:, g, part(c, K_PASS)],
                 in0=bank[:],
                 scalar=q_sq_half[:, g : g + 1],
-                in1=k_sq_half[:, block(c, K_PASS)],
+                in1=k_sq_half[:, part(c, K_PASS)],
                 op0=ALU.subtract,
                 op1=ALU.subtract,
             )
@@ -214,41 +219,42 @@ def tile_attention_pa_kernel(tc, q, k, x, Wv, out):
                 op1=ALU.add,
             )
 
-        def value_block(c, r, copy):
+        def value_columns(c, r, copy):
             bank = psum.tile([P, PACK, P], F32, tag="tp")
             for t in range(PACK):
-                multiply(nc, bank[:, t, :], x_mx, block(c * PACK + t, P), w_mx, block(r, P), True, True)
+                multiply(nc, bank[:, t, :], x_mx, part(c * PACK + t, P), w_mx, part(r, P), True, True)
             copy(
-                out=v_mx[0][:, block(c * PACK + r, P), :], in_=bank[:].rearrange("p t d -> p d t")
+                out=v_mx[0][:, part(c * PACK + r, P), :], in_=bank[:].rearrange("p t d -> p d t")
             )
 
         late = ((q_rows, q_mx, 1), (w_rows, w_mx, 0), (x_rows, x_mx, 0), (x_rows, x_mx, 1))
-        banks = {0: products(0), 1: products(1)}
-        subtract(0, 0, banks[0][0])
-        subtract(0, 1, banks[0][1])
+        qk_of = {0: products(0), 1: products(1)}
+        subtract(0, 0, qk_of[0][0])
+        subtract(0, 1, qk_of[0][1])
+        quantise(nc, q_mx, part(1, 2 * P))
         for g in range(TILES):
             if g + 3 < TILES:
                 query_squares(g + 3)
             if g < len(late):
                 rows, operand, c = late[g]
-                features_to_partitions(rows, operand, c, nc.scalar.copy)
+                features_to_partitions(rows, operand, c, BOTH, nc.scalar.copy)
             else:
-                value_block(0, g - len(late), nc.scalar.copy)
+                value_columns(0, g - len(late), nc.scalar.copy)
             if g + 2 < TILES:
-                banks[g + 2] = products(g + 2)
+                qk_of[g + 2] = products(g + 2)
             if g + 1 < TILES:
-                subtract(g + 1, 0, banks[g + 1][0])
+                subtract(g + 1, 0, qk_of[g + 1][0])
             clamp(g)
             if g + 1 < TILES:
-                subtract(g + 1, 1, banks[g + 1][1])
+                subtract(g + 1, 1, qk_of[g + 1][1])
             if g < len(late) - 1:
-                quantise(nc, operand, block(c, K_PASS))
+                quantise(nc, operand, part(c, K_PASS))
             roots(g)
 
-        quantise(nc, x_mx, block(1, K_PASS))
-        quantise(nc, v_mx, block(0, FEATS))
+        quantise(nc, x_mx, part(1, K_PASS))
+        quantise(nc, v_mx, part(0, FEATS))
         for r in range(PACK):
-            value_block(1, r, nc.vector.tensor_copy)
+            value_columns(1, r, nc.vector.tensor_copy)
 
         def weights(g):
             e_rows = work.tile([P, TOKENS], BF16, tag="e_rows")
@@ -262,7 +268,7 @@ def tile_attention_pa_kernel(tc, q, k, x, Wv, out):
             )
             bank = psum.tile([P, TILES, P], BF16, tag="tp")
             for j in range(TILES):
-                nc.tensor.transpose(bank[:, j, :], e_rows[:, block(j, P)], ident_bf16[:])
+                nc.tensor.transpose(bank[:, j, :], e_rows[:, part(j, P)], ident_bf16[:])
             e_grouped = work.tile([P, CHUNKS * P, PACK], BF16, tag="e_grouped", align_bytes=64)
             if g % PACK == PACK - 1:
                 nc.vector.reciprocal(
@@ -278,13 +284,13 @@ def tile_attention_pa_kernel(tc, q, k, x, Wv, out):
             e_codes = work.tile([P, CHUNKS * P], U32, tag="e_codes", align_bytes=64)
             e_scales = work.tile([P, CHUNKS * P], U8, tag="e_scales", align_bytes=64)
             e_mx = (e_grouped, e_codes, e_scales)
-            quantise(nc, e_mx, block(0, CHUNKS * P))
+            quantise(nc, e_mx, part(0, CHUNKS * P))
             return e_mx
 
         def weighted_sum(e_mx):
             acc = psum.tile([P, FEATS], F32, tag="mm")
             for c in range(CHUNKS):
-                multiply(nc, acc[:], e_mx, block(c, P), v_mx, block(c, FEATS), c == 0, c == CHUNKS - 1)
+                multiply(nc, acc[:], e_mx, part(c, P), v_mx, part(c, FEATS), c == 0, c == CHUNKS - 1)
             return acc
 
         def finish(g, acc):
@@ -301,7 +307,7 @@ def tile_attention_pa_kernel(tc, q, k, x, Wv, out):
             if step < TILES:
                 grouped_of[step] = weights(step)
             if step == 0:
-                quantise(nc, v_mx, block(1, FEATS))
+                quantise(nc, v_mx, part(1, FEATS))
             if 0 <= step - QUANTISE_LAG < TILES:
                 e_of[step - QUANTISE_LAG] = quantise_weights(grouped_of[step - QUANTISE_LAG])
             if 0 <= step - MULTIPLY_LAG < TILES:

@@ -88,8 +88,6 @@ def tile_attention_pa_kernel(tc, q, k, x, Wv, out):
 
         ident_f32 = keep.tile([P, P], F32, name="ident_f32")
         make_identity(nc, ident_f32[:])
-        ident_bf16 = keep.tile([P, P], BF16, name="ident_bf16")
-        make_identity(nc, ident_bf16[:])
 
         one = keep.tile([P, 1], F32, name="one")
         nc.vector.memset(one[:], 1.0)
@@ -121,7 +119,7 @@ def tile_attention_pa_kernel(tc, q, k, x, Wv, out):
                 accum_out=sums[:, g : g + 1],
             )
 
-        def features_to_partitions(rows, operand, c, pairs, copy):
+        def features_to_partitions(rows, operand, c, pairs, copy, interleave=False):
             words = rows[:].bitcast(F32)
             grouped_words = operand[0][:].bitcast(F32)
             for pair in pairs:
@@ -131,10 +129,14 @@ def tile_attention_pa_kernel(tc, q, k, x, Wv, out):
                         nc.tensor.transpose(
                             bank[:, u, part(a, P)], words[:, c, 2 * pair + a, part(u, P)], ident_f32[:]
                         )
-                copy(
-                    out=grouped_words[:, part(2 * c + pair, 2 * P), :],
-                    in_=bank[:].rearrange("p u m -> p m u"),
-                )
+                cols = grouped_words[:, part(2 * c + pair, 2 * P), :]
+                if interleave:
+                    copy(
+                        out=cols.rearrange("p (m a) u -> p m a u", a=2),
+                        in_=bank[:].rearrange("p u (a m) -> p m a u", a=2),
+                    )
+                else:
+                    copy(out=cols, in_=bank[:].rearrange("p u m -> p m u"))
 
         def spread_key_squares(c):
             bank = psum.tile([P, PACK, P], F32, tag="tp")
@@ -143,7 +145,7 @@ def tile_attention_pa_kernel(tc, q, k, x, Wv, out):
                 nc.tensor.transpose(
                     bank[:, t, :], k_sq[:, g : g + 1].to_broadcast([P, P]), ident_f32[:]
                 )
-            return bank[:].rearrange("p t m -> p (t m)")
+            return bank[:].rearrange("p (u e) m -> p u m e", e=2)
 
         def query_squares(g):
             sum_of_squares(q_rows, q_sq, g)
@@ -158,18 +160,19 @@ def tile_attention_pa_kernel(tc, q, k, x, Wv, out):
 
         for g in range(PACK):
             sum_of_squares(k_rows, k_sq, g)
-        features_to_partitions(k_rows, k_mx, 0, BOTH, nc.vector.tensor_copy)
+        features_to_partitions(k_rows, k_mx, 0, BOTH, nc.vector.tensor_copy, True)
         for g in range(PACK, TILES):
             sum_of_squares(k_rows, k_sq, g)
-        features_to_partitions(k_rows, k_mx, 1, BOTH, nc.vector.tensor_copy)
+        features_to_partitions(k_rows, k_mx, 1, BOTH, nc.vector.tensor_copy, True)
         quantise(nc, k_mx, part(0, K_PASS))
         spread_0 = spread_key_squares(0)
         query_squares(0)
         features_to_partitions(q_rows, q_mx, 0, (0,), nc.vector.tensor_copy)
         quantise(nc, k_mx, part(1, K_PASS))
         quantise(nc, q_mx, part(0, 2 * P))
-        nc.vector.tensor_scalar_mul(out=k_sq_half[:, part(0, K_PASS)], in0=spread_0, scalar1=0.5)
-        nc.scalar.mul(out=k_sq_half[:, part(1, K_PASS)], in_=spread_key_squares(1), mul=0.5)
+        half_view = k_sq_half[:].rearrange("p (c u m e) -> p c u m e", c=CHUNKS, u=2, e=2)
+        nc.vector.tensor_scalar_mul(out=half_view[:, 0], in0=spread_0, scalar1=0.5)
+        nc.scalar.mul(out=half_view[:, 1], in_=spread_key_squares(1), mul=0.5)
         query_squares(1)
         features_to_partitions(q_rows, q_mx, 0, (1,), nc.scalar.copy)
         query_squares(2)
@@ -266,17 +269,18 @@ def tile_attention_pa_kernel(tc, q, k, x, Wv, out):
                 scale=1.0,
                 accum_out=row_sum[:, g : g + 1],
             )
-            bank = psum.tile([P, TILES, P], BF16, tag="tp")
-            for j in range(TILES):
-                nc.tensor.transpose(bank[:, j, :], e_rows[:, part(j, P)], ident_bf16[:])
+            words = e_rows[:].bitcast(F32)
+            bank = psum.tile([P, 2 * CHUNKS, P], F32, tag="tp")
+            for j in range(2 * CHUNKS):
+                nc.tensor.transpose(bank[:, j, :], words[:, part(j, P)], ident_f32[:])
             e_grouped = work.tile([P, CHUNKS * P, PACK], BF16, tag="e_grouped", align_bytes=64)
             if g % PACK == PACK - 1:
                 nc.vector.reciprocal(
                     out=row_inv[:, g + 1 - PACK : g + 1], in_=row_sum[:, g + 1 - PACK : g + 1]
                 )
             nc.vector.tensor_copy(
-                out=e_grouped[:].rearrange("p (c i) t -> p c i t", c=CHUNKS),
-                in_=bank[:].rearrange("p (c t) i -> p c i t", c=CHUNKS),
+                out=e_grouped[:].bitcast(F32).rearrange("p (c i) u -> p c i u", c=CHUNKS),
+                in_=bank[:].rearrange("p (c u) i -> p c i u", c=CHUNKS),
             )
             return e_grouped
 

@@ -24,7 +24,6 @@ ROW = TOKENS + 8
 
 QUANTISE_LAG = 1
 MULTIPLY_LAG = 2
-FINISH_LAG = 5
 
 FLOPS = 2 * TOKENS * FEATS * FEATS + 2 * 2 * TOKENS * TOKENS * FEATS
 
@@ -77,7 +76,7 @@ def tile_attention_pa_kernel(tc, q, k, x, Wv, out):
         ctx.enter_context(tc.manual_schedule())
         keep = ctx.enter_context(tc.tile_pool(name="keep", bufs=1))
         work = ctx.enter_context(tc.tile_pool(name="work", bufs=3))
-        results = ctx.enter_context(tc.tile_pool(name="results", bufs=4))
+        results = ctx.enter_context(tc.tile_pool(name="results", bufs=TILES))
         psum = ctx.enter_context(tc.psum_pool(name="psum", bufs=4))
 
         k_rows = load_tokens(nc, keep, k, "k_rows", 2)
@@ -274,9 +273,9 @@ def tile_attention_pa_kernel(tc, q, k, x, Wv, out):
             for j in range(2 * CHUNKS):
                 nc.tensor.transpose(bank[:, j, :], words[:, part(j, P)], ident_f32[:])
             e_grouped = work.tile([P, CHUNKS * P, PACK], BF16, tag="e_grouped", align_bytes=64)
-            if g % PACK == PACK - 1:
+            if g % 2 == 1:
                 nc.vector.reciprocal(
-                    out=row_inv[:, g + 1 - PACK : g + 1], in_=row_sum[:, g + 1 - PACK : g + 1]
+                    out=row_inv[:, g - 1 : g + 1], in_=row_sum[:, g - 1 : g + 1]
                 )
             nc.vector.tensor_copy(
                 out=e_grouped[:].bitcast(F32).rearrange("p (c i) u -> p c i u", c=CHUNKS),
@@ -297,24 +296,40 @@ def tile_attention_pa_kernel(tc, q, k, x, Wv, out):
                 multiply(nc, acc[:], e_mx, part(c, P), v_mx, part(c, FEATS), c == 0, c == CHUNKS - 1)
             return acc
 
-        def finish(g, acc):
+        def finish(g, acc, split):
             result = results.tile([P, FEATS], F32, tag="result")
-            nc.scalar.activation(
-                out=result[:], in_=acc[:], func=ACT.Copy, scale=row_inv[:, g : g + 1]
-            )
+            inverse = row_inv[:, g : g + 1]
+            if split > 0:
+                nc.scalar.activation(
+                    out=result[:, :split], in_=acc[:, :split], func=ACT.Copy, scale=inverse
+                )
+            if split < FEATS:
+                nc.vector.tensor_scalar_mul(
+                    out=result[:, split:], in0=acc[:, split:], scalar1=inverse
+                )
             nc.sync.dma_start(out=out_view[:, g // PACK, g % PACK, :], in_=result[:])
 
         grouped_of = {}
         e_of = {}
         acc_of = {}
-        for step in range(TILES + FINISH_LAG):
+        for step in range(TILES + MULTIPLY_LAG):
             if step < TILES:
                 grouped_of[step] = weights(step)
             if step == 0:
                 quantise(nc, v_mx, part(1, FEATS))
             if 0 <= step - QUANTISE_LAG < TILES:
                 e_of[step - QUANTISE_LAG] = quantise_weights(grouped_of[step - QUANTISE_LAG])
+            if step == 4:
+                finish(0, acc_of[0], 0)
+            if step == 6:
+                finish(1, acc_of[1], 0)
+            if step == 7:
+                finish(2, acc_of[2], FEATS)
+                finish(3, acc_of[3], FEATS)
             if 0 <= step - MULTIPLY_LAG < TILES:
                 acc_of[step - MULTIPLY_LAG] = weighted_sum(e_of[step - MULTIPLY_LAG])
-            if step >= FINISH_LAG:
-                finish(step - FINISH_LAG, acc_of[step - FINISH_LAG])
+            if step == 8:
+                finish(4, acc_of[4], FEATS)
+                finish(5, acc_of[5], FEATS)
+        finish(6, acc_of[6], 0)
+        finish(7, acc_of[7], FEATS // 2)

@@ -22,9 +22,6 @@ BOTH = (0, 1)
 HALVES = FEATS // 2 // P
 ROW = TOKENS + 8
 
-QUANTISE_LAG = 1
-MULTIPLY_LAG = 2
-
 FLOPS = 2 * TOKENS * FEATS * FEATS + 2 * 2 * TOKENS * TOKENS * FEATS
 
 
@@ -77,6 +74,7 @@ def tile_attention_pa_kernel(tc, q, k, x, Wv, out):
         keep = ctx.enter_context(tc.tile_pool(name="keep", bufs=1))
         work = ctx.enter_context(tc.tile_pool(name="work", bufs=3))
         results = ctx.enter_context(tc.tile_pool(name="results", bufs=TILES))
+        quantised = ctx.enter_context(tc.tile_pool(name="quantised", bufs=5))
         psum = ctx.enter_context(tc.psum_pool(name="psum", bufs=4))
 
         k_rows = load_tokens(nc, keep, k, "k_rows", 2)
@@ -257,79 +255,92 @@ def tile_attention_pa_kernel(tc, q, k, x, Wv, out):
         quantise(nc, v_mx, part(0, FEATS))
         for r in range(PACK):
             value_columns(1, r, nc.vector.tensor_copy)
+        quantise(nc, v_mx, part(1, FEATS))
 
-        def weights(g):
-            e_rows = work.tile([P, TOKENS], BF16, tag="e_rows")
+        def exps(g, e_rows, cols, sums):
             nc.scalar.activation(
-                out=e_rows[:],
-                in_=scores[:, g, 0:TOKENS],
+                out=e_rows[:, cols],
+                in_=scores[:, g, cols],
                 func=ACT.Exp,
                 bias=neg_max[:, g : g + 1],
                 scale=1.0,
-                accum_out=row_sum[:, g : g + 1],
+                accum_out=sums,
             )
+
+        def keys_to_partitions(e_rows, e_grouped, chunks):
             words = e_rows[:].bitcast(F32)
-            bank = psum.tile([P, 2 * CHUNKS, P], F32, tag="tp")
-            for j in range(2 * CHUNKS):
-                nc.tensor.transpose(bank[:, j, :], words[:, part(j, P)], ident_f32[:])
-            e_grouped = work.tile([P, CHUNKS * P, PACK], BF16, tag="e_grouped", align_bytes=64)
-            if g % 2 == 1:
-                nc.vector.reciprocal(
-                    out=row_inv[:, g - 1 : g + 1], in_=row_sum[:, g - 1 : g + 1]
-                )
+            bank = psum.tile([P, len(chunks), 2, P], F32, tag="tp")
+            for i, c in enumerate(chunks):
+                for u in range(2):
+                    nc.tensor.transpose(bank[:, i, u, :], words[:, part(2 * c + u, P)], ident_f32[:])
+            grouped_words = e_grouped[:].bitcast(F32).rearrange("p (c i) u -> p c i u", c=CHUNKS)
             nc.vector.tensor_copy(
-                out=e_grouped[:].bitcast(F32).rearrange("p (c i) u -> p c i u", c=CHUNKS),
-                in_=bank[:].rearrange("p (c u) i -> p c i u", c=CHUNKS),
+                out=grouped_words[:, chunks[0] : chunks[-1] + 1],
+                in_=bank[:].rearrange("p c u i -> p c i u"),
             )
-            return e_grouped
 
-        def quantise_weights(e_grouped):
-            e_codes = work.tile([P, CHUNKS * P], U32, tag="e_codes", align_bytes=64)
-            e_scales = work.tile([P, CHUNKS * P], U8, tag="e_scales", align_bytes=64)
-            e_mx = (e_grouped, e_codes, e_scales)
-            quantise(nc, e_mx, part(0, CHUNKS * P))
-            return e_mx
+        def invert_sums(tiles):
+            nc.vector.reciprocal(out=row_inv[:, tiles], in_=row_sum[:, tiles])
 
-        def weighted_sum(e_mx):
-            acc = psum.tile([P, FEATS], F32, tag="mm")
+        def weight_tiles():
+            e_rows = work.tile([P, TOKENS], BF16, tag="e_rows")
+            e_grouped = work.tile([P, CHUNKS * P, PACK], BF16, tag="e_grouped", align_bytes=64)
+            e_codes = quantised.tile([P, CHUNKS * P], U32, tag="e_codes", align_bytes=64)
+            e_scales = quantised.tile([P, CHUNKS * P], U8, tag="e_scales", align_bytes=64)
+            return e_rows, (e_grouped, e_codes, e_scales)
+
+        def weighted_sum(e_mx, cols):
+            acc = psum.tile([P, cols.stop - cols.start], F32, tag="mm")
             for c in range(CHUNKS):
-                multiply(nc, acc[:], e_mx, part(c, P), v_mx, part(c, FEATS), c == 0, c == CHUNKS - 1)
+                v_cols = slice(c * FEATS + cols.start, c * FEATS + cols.stop)
+                multiply(nc, acc[:], e_mx, part(c, P), v_mx, v_cols, c == 0, c == CHUNKS - 1)
             return acc
 
-        def finish(g, acc, split):
-            result = results.tile([P, FEATS], F32, tag="result")
+        def finish(g, cols, acc, on_scalar):
+            result = results.tile([P, cols.stop - cols.start], F32, tag="result")
             inverse = row_inv[:, g : g + 1]
-            if split > 0:
-                nc.scalar.activation(
-                    out=result[:, :split], in_=acc[:, :split], func=ACT.Copy, scale=inverse
-                )
-            if split < FEATS:
-                nc.vector.tensor_scalar_mul(
-                    out=result[:, split:], in0=acc[:, split:], scalar1=inverse
-                )
-            nc.sync.dma_start(out=out_view[:, g // PACK, g % PACK, :], in_=result[:])
+            if on_scalar:
+                nc.scalar.activation(out=result[:], in_=acc[:], func=ACT.Copy, scale=inverse)
+            else:
+                nc.vector.tensor_scalar_mul(out=result[:], in0=acc[:], scalar1=inverse)
+            nc.sync.dma_start(out=out_view[:, g // PACK, g % PACK, cols], in_=result[:])
 
-        grouped_of = {}
+        every = slice(0, FEATS)
+        last = TILES - 1
         e_of = {}
         acc_of = {}
-        for step in range(TILES + MULTIPLY_LAG):
-            if step < TILES:
-                grouped_of[step] = weights(step)
-            if step == 0:
-                quantise(nc, v_mx, part(1, FEATS))
-            if 0 <= step - QUANTISE_LAG < TILES:
-                e_of[step - QUANTISE_LAG] = quantise_weights(grouped_of[step - QUANTISE_LAG])
-            if step == 4:
-                finish(0, acc_of[0], 0)
-            if step == 6:
-                finish(1, acc_of[1], 0)
-            if step == 7:
-                finish(2, acc_of[2], FEATS)
-                finish(3, acc_of[3], FEATS)
-            if 0 <= step - MULTIPLY_LAG < TILES:
-                acc_of[step - MULTIPLY_LAG] = weighted_sum(e_of[step - MULTIPLY_LAG])
-            if step == 8:
-                finish(4, acc_of[4], FEATS)
-                finish(5, acc_of[5], FEATS)
-        finish(6, acc_of[6], 0)
-        finish(7, acc_of[7], FEATS // 2)
+        for g in range(last):
+            e_rows, e_of[g] = weight_tiles()
+            exps(g, e_rows, slice(0, TOKENS), row_sum[:, g : g + 1])
+            keys_to_partitions(e_rows, e_of[g][0], BOTH)
+            if g >= 3:
+                acc_of[g - 3] = weighted_sum(e_of[g - 3], every)
+            if g >= 1:
+                quantise(nc, e_of[g - 1], part(0, CHUNKS * P))
+            if g in (2, 4, 6):
+                invert_sums(slice(g - 2, g))
+            if g in (4, 5):
+                finish(g - 4, every, acc_of[g - 4], False)
+        e_rows, e_of[last] = weight_tiles()
+        halves = keep.tile([P, CHUNKS], F32, name="halves")
+        for c in range(CHUNKS):
+            exps(last, e_rows, part(c, K_PASS), halves[:, c : c + 1])
+            keys_to_partitions(e_rows, e_of[last][0], (c,))
+            if c == 0:
+                acc_of[4] = weighted_sum(e_of[4], every)
+                quantise(nc, e_of[last - 1], part(0, CHUNKS * P))
+        acc_of[5] = weighted_sum(e_of[5], every)
+        nc.vector.tensor_add(out=row_sum[:, last:], in0=halves[:, 0:1], in1=halves[:, 1:2])
+        quantise(nc, e_of[last], part(0, P))
+        quantise(nc, e_of[last], part(1, P))
+        invert_sums(slice(last - 1, TILES))
+        finish(2, every, acc_of[2], True)
+        acc_of[last - 1] = weighted_sum(e_of[last - 1], every)
+        finish(3, every, acc_of[3], True)
+        left = weighted_sum(e_of[last], part(0, FEATS // 2))
+        finish(4, every, acc_of[4], True)
+        right = weighted_sum(e_of[last], part(1, FEATS // 2))
+        finish(5, every, acc_of[5], True)
+        finish(6, every, acc_of[6], False)
+        finish(last, part(0, FEATS // 2), left, False)
+        finish(last, part(1, FEATS // 2), right, True)

@@ -33,8 +33,8 @@ def load_tokens(nc, pool, src, name, tiles_a_load):
     rows = pool.tile([P, CHUNKS, PACK, FEATS], BF16, name=name)
     view = src.flatten_outer_dims().rearrange("(c p t) f -> p c t f", p=P, t=PACK)
     for c in range(CHUNKS):
-        for i in range(PACK // tiles_a_load):
-            tiles = part(i, tiles_a_load)
+        for i in range(PACK // tiles_a_load[c]):
+            tiles = part(i, tiles_a_load[c])
             nc.sync.dma_start(out=rows[:, c, tiles], in_=view[:, c, tiles])
     return rows
 
@@ -77,11 +77,11 @@ def tile_attention_pa_kernel(tc, q, k, x, Wv, out):
         quantised = ctx.enter_context(tc.tile_pool(name="quantised", bufs=5))
         psum = ctx.enter_context(tc.psum_pool(name="psum", bufs=4))
 
-        k_rows = load_tokens(nc, keep, k, "k_rows", 2)
-        q_rows = load_tokens(nc, keep, q, "q_rows", PACK)
+        k_rows = load_tokens(nc, keep, k, "k_rows", (2, 2))
+        q_rows = load_tokens(nc, keep, q, "q_rows", (2, PACK))
         w_rows = keep.tile([P, 1, FEATS // P, FEATS], BF16, name="w_rows")
         nc.sync.dma_start(out=w_rows[:, 0], in_=Wv.rearrange("(r p) f -> p r f", p=P))
-        x_rows = load_tokens(nc, keep, x, "x_rows", PACK)
+        x_rows = load_tokens(nc, keep, x, "x_rows", (PACK, PACK))
 
         ident_f32 = keep.tile([P, P], F32, name="ident_f32")
         make_identity(nc, ident_f32[:])
@@ -155,21 +155,30 @@ def tile_attention_pa_kernel(tc, q, k, x, Wv, out):
                 op1=ALU.add,
             )
 
-        for g in range(PACK):
+        row = k_rows[:, 0, 0, :]
+        squares = keep.tile([P, FEATS], BF16, name="first_squares")
+        nc.vector.scalar_tensor_tensor(
+            out=squares[:],
+            in0=row,
+            scalar=1.0,
+            in1=row,
+            op0=ALU.mult,
+            op1=ALU.mult,
+            accum_out=k_sq[:, 0:1],
+        )
+        for g in range(1, TILES):
             sum_of_squares(k_rows, k_sq, g)
         features_to_partitions(k_rows, k_mx, 0, BOTH, nc.vector.tensor_copy, True)
-        for g in range(PACK, TILES):
-            sum_of_squares(k_rows, k_sq, g)
-        features_to_partitions(k_rows, k_mx, 1, BOTH, nc.vector.tensor_copy, True)
-        quantise(nc, k_mx, part(0, K_PASS))
-        spread_0 = spread_key_squares(0)
+        features_to_partitions(k_rows, k_mx, 1, (0,), nc.vector.tensor_copy, True)
+        features_to_partitions(k_rows, k_mx, 1, (1,), nc.scalar.copy, True)
         query_squares(0)
+        quantise(nc, k_mx, part(0, K_PASS))
         features_to_partitions(q_rows, q_mx, 0, (0,), nc.vector.tensor_copy)
-        quantise(nc, k_mx, part(1, K_PASS))
-        quantise(nc, q_mx, part(0, 2 * P))
         half_view = k_sq_half[:].rearrange("p (c u m e) -> p c u m e", c=CHUNKS, u=2, e=2)
-        nc.vector.tensor_scalar_mul(out=half_view[:, 0], in0=spread_0, scalar1=0.5)
+        nc.vector.tensor_scalar_mul(out=half_view[:, 0], in0=spread_key_squares(0), scalar1=0.5)
         nc.scalar.mul(out=half_view[:, 1], in_=spread_key_squares(1), mul=0.5)
+        quantise(nc, q_mx, part(0, 2 * P))
+        quantise(nc, k_mx, part(1, K_PASS))
         query_squares(1)
         features_to_partitions(q_rows, q_mx, 0, (1,), nc.scalar.copy)
         query_squares(2)
@@ -192,31 +201,20 @@ def tile_attention_pa_kernel(tc, q, k, x, Wv, out):
                 op1=ALU.subtract,
             )
 
-        def clamp(g):
+        def clamp(g, cols, smallest):
             nc.vector.tensor_scalar(
-                out=scores[:, g, 0:TOKENS],
-                in0=scores[:, g, 0:TOKENS],
+                out=scores[:, g, cols],
+                in0=scores[:, g, cols],
                 scalar1=0.0,
                 scalar2=None,
                 op0=ALU.min,
                 op1=ALU.min,
-                accum_out=scores[:, g, TOKENS : TOKENS + 1],
+                accum_out=scores[:, g, smallest : smallest + 1],
             )
 
-        def roots(g):
+        def roots(g, cols):
             nc.scalar.activation(
-                out=scores[:, g, 0 : TOKENS + 1],
-                in_=scores[:, g, 0 : TOKENS + 1],
-                func=ACT.Sqrt,
-                scale=-2.0 / FEATS,
-            )
-            nc.gpsimd.tensor_scalar(
-                out=neg_max[:, g : g + 1],
-                in0=scores[:, g, TOKENS : TOKENS + 1],
-                scalar1=-1.0,
-                scalar2=0.0,
-                op0=ALU.mult,
-                op1=ALU.add,
+                out=scores[:, g, cols], in_=scores[:, g, cols], func=ACT.Sqrt, scale=-2.0 / FEATS
             )
 
         def value_columns(c, r, copy):
@@ -227,6 +225,7 @@ def tile_attention_pa_kernel(tc, q, k, x, Wv, out):
                 out=v_mx[0][:, part(c * PACK + r, P), :], in_=bank[:].rearrange("p t d -> p d t")
             )
 
+        every_key = slice(0, TOKENS)
         late = ((q_rows, q_mx, 1), (w_rows, w_mx, 0), (x_rows, x_mx, 0), (x_rows, x_mx, 1))
         qk_of = {0: products(0), 1: products(1)}
         subtract(0, 0, qk_of[0][0])
@@ -244,12 +243,35 @@ def tile_attention_pa_kernel(tc, q, k, x, Wv, out):
                 qk_of[g + 2] = products(g + 2)
             if g + 1 < TILES:
                 subtract(g + 1, 0, qk_of[g + 1][0])
-            clamp(g)
+            if g + 1 < TILES:
+                clamp(g, every_key, TOKENS)
             if g + 1 < TILES:
                 subtract(g + 1, 1, qk_of[g + 1][1])
             if g < len(late) - 1:
                 quantise(nc, operand, part(c, K_PASS))
-            roots(g)
+            if g + 1 < TILES:
+                roots(g, slice(0, TOKENS + 1))
+                nc.gpsimd.tensor_scalar(
+                    out=neg_max[:, g : g + 1],
+                    in0=scores[:, g, TOKENS : TOKENS + 1],
+                    scalar1=-1.0,
+                    scalar2=0.0,
+                    op0=ALU.mult,
+                    op1=ALU.add,
+                )
+        last = TILES - 1
+        clamp(last, part(0, K_PASS), TOKENS)
+        clamp(last, part(1, K_PASS), TOKENS + 1)
+        roots(last, part(0, K_PASS))
+        roots(last, slice(K_PASS, TOKENS + 2))
+        nc.gpsimd.tensor_scalar(
+            out=neg_max[:, last : last + 1],
+            in0=scores[:, last, TOKENS : TOKENS + 1],
+            scalar1=scores[:, last, TOKENS + 1 : TOKENS + 2],
+            scalar2=-1.0,
+            op0=ALU.max,
+            op1=ALU.mult,
+        )
 
         quantise(nc, x_mx, part(1, K_PASS))
         quantise(nc, v_mx, part(0, FEATS))
@@ -306,7 +328,6 @@ def tile_attention_pa_kernel(tc, q, k, x, Wv, out):
             nc.sync.dma_start(out=out_view[:, g // PACK, g % PACK, cols], in_=result[:])
 
         every = slice(0, FEATS)
-        last = TILES - 1
         e_of = {}
         acc_of = {}
         for g in range(last):

@@ -86,6 +86,14 @@ def tile_attention_pa_kernel(tc, q, k, x, Wv, out):
         ident_f32 = keep.tile([P, P], F32, name="ident_f32")
         make_identity(nc, ident_f32[:])
 
+        zeros = keep.tile([P, FEATS], BF16, name="zeros")
+        nc.gpsimd.memset(zeros[:], 0.0)
+
+        def spin(passes):
+            bank = psum.tile([P, FEATS], F32, tag="mm")
+            for i in range(passes):
+                nc.tensor.matmul(bank[:], lhsT=zeros[:, 0:P], rhs=zeros[:], start=True, stop=True)
+
         one = keep.tile([P, 1], F32, name="one")
         nc.vector.memset(one[:], 1.0)
         warm = keep.tile([P, 1], F32, name="warm")
@@ -99,8 +107,8 @@ def tile_attention_pa_kernel(tc, q, k, x, Wv, out):
 
         k_sq = keep.tile([P, TILES], F32, name="k_sq")
         q_sq = keep.tile([P, TILES], F32, name="q_sq")
-        q_sq_half = keep.tile([P, TILES], F32, name="q_sq_half")
-        k_sq_half = keep.tile([P, TOKENS], F32, name="k_sq_half")
+        q_sq_scaled = keep.tile([P, TILES], F32, name="q_sq_scaled")
+        k_sq_row = keep.tile([P, TOKENS], F32, name="k_sq_row")
         scores = keep.tile([P, TILES, ROW], F32, name="scores")
         neg_max = keep.tile([P, TILES], F32, name="neg_max")
         row_sum = keep.tile([P, TILES], F32, name="row_sum")
@@ -147,40 +155,41 @@ def tile_attention_pa_kernel(tc, q, k, x, Wv, out):
         def query_squares(g):
             sum_of_squares(q_rows, q_sq, g)
             nc.gpsimd.tensor_scalar(
-                out=q_sq_half[:, g : g + 1],
+                out=q_sq_scaled[:, g : g + 1],
                 in0=q_sq[:, g : g + 1],
-                scalar1=0.5,
+                scalar1=1.0 / FEATS,
                 scalar2=0.0,
                 op0=ALU.mult,
                 op1=ALU.add,
             )
 
-        row = k_rows[:, 0, 0, :]
-        squares = keep.tile([P, FEATS], BF16, name="first_squares")
-        nc.vector.scalar_tensor_tensor(
-            out=squares[:],
-            in0=row,
-            scalar=1.0,
-            in1=row,
-            op0=ALU.mult,
-            op1=ALU.mult,
-            accum_out=k_sq[:, 0:1],
-        )
-        for g in range(1, TILES):
+        for g in range(2):
+            row = k_rows[:, 0, g, :]
+            squares = work.tile([P, FEATS], BF16, tag="first_squares")
+            nc.vector.scalar_tensor_tensor(
+                out=squares[:],
+                in0=row,
+                scalar=1.0,
+                in1=row,
+                op0=ALU.mult,
+                op1=ALU.mult,
+                accum_out=k_sq[:, g : g + 1],
+            )
+        for g in range(2, TILES):
             sum_of_squares(k_rows, k_sq, g)
         features_to_partitions(k_rows, k_mx, 0, BOTH, nc.vector.tensor_copy, True)
         features_to_partitions(k_rows, k_mx, 1, (0,), nc.vector.tensor_copy, True)
         features_to_partitions(k_rows, k_mx, 1, (1,), nc.scalar.copy, True)
-        query_squares(0)
         quantise(nc, k_mx, part(0, K_PASS))
         features_to_partitions(q_rows, q_mx, 0, (0,), nc.vector.tensor_copy)
-        half_view = k_sq_half[:].rearrange("p (c u m e) -> p c u m e", c=CHUNKS, u=2, e=2)
-        nc.vector.tensor_scalar_mul(out=half_view[:, 0], in0=spread_key_squares(0), scalar1=0.5)
-        nc.scalar.mul(out=half_view[:, 1], in_=spread_key_squares(1), mul=0.5)
+        row_view = k_sq_row[:].rearrange("p (c u m e) -> p c u m e", c=CHUNKS, u=2, e=2)
+        nc.vector.tensor_copy(out=row_view[:, 0], in_=spread_key_squares(0))
+        nc.scalar.copy(out=row_view[:, 1], in_=spread_key_squares(1))
         quantise(nc, q_mx, part(0, 2 * P))
         quantise(nc, k_mx, part(1, K_PASS))
-        query_squares(1)
+        query_squares(0)
         features_to_partitions(q_rows, q_mx, 0, (1,), nc.scalar.copy)
+        query_squares(1)
         query_squares(2)
 
         def products(g):
@@ -195,9 +204,9 @@ def tile_attention_pa_kernel(tc, q, k, x, Wv, out):
             nc.vector.scalar_tensor_tensor(
                 out=scores[:, g, part(c, K_PASS)],
                 in0=bank[:],
-                scalar=q_sq_half[:, g : g + 1],
-                in1=k_sq_half[:, part(c, K_PASS)],
-                op0=ALU.subtract,
+                scalar=2.0,
+                in1=k_sq_row[:, part(c, K_PASS)],
+                op0=ALU.mult,
                 op1=ALU.subtract,
             )
 
@@ -205,7 +214,7 @@ def tile_attention_pa_kernel(tc, q, k, x, Wv, out):
             nc.vector.tensor_scalar(
                 out=scores[:, g, cols],
                 in0=scores[:, g, cols],
-                scalar1=0.0,
+                scalar1=q_sq[:, g : g + 1],
                 scalar2=None,
                 op0=ALU.min,
                 op1=ALU.min,
@@ -214,7 +223,11 @@ def tile_attention_pa_kernel(tc, q, k, x, Wv, out):
 
         def roots(g, cols):
             nc.scalar.activation(
-                out=scores[:, g, cols], in_=scores[:, g, cols], func=ACT.Sqrt, scale=-2.0 / FEATS
+                out=scores[:, g, cols],
+                in_=scores[:, g, cols],
+                func=ACT.Sqrt,
+                bias=q_sq_scaled[:, g : g + 1],
+                scale=-1.0 / FEATS,
             )
 
         def value_columns(c, r, copy):
@@ -277,6 +290,7 @@ def tile_attention_pa_kernel(tc, q, k, x, Wv, out):
         quantise(nc, v_mx, part(0, FEATS))
         for r in range(PACK):
             value_columns(1, r, nc.vector.tensor_copy)
+        spin(2)
         quantise(nc, v_mx, part(1, FEATS))
 
         def exps(g, e_rows, cols, sums):
@@ -336,6 +350,8 @@ def tile_attention_pa_kernel(tc, q, k, x, Wv, out):
             keys_to_partitions(e_rows, e_of[g][0], BOTH)
             if g >= 3:
                 acc_of[g - 3] = weighted_sum(e_of[g - 3], every)
+            else:
+                spin(2)
             if g >= 1:
                 quantise(nc, e_of[g - 1], part(0, CHUNKS * P))
             if g in (2, 4, 6):

@@ -210,6 +210,13 @@ def tile_attention_pa_kernel(tc, q, k, x, Wv, out):
                 op1=ALU.subtract,
             )
 
+        def subtract_beside(g, c, bank):
+            cols = scores[:, g, part(c, K_PASS)]
+            nc.scalar.activation(out=cols, in_=bank[:], func=ACT.Copy, scale=2.0)
+            nc.gpsimd.tensor_tensor(
+                out=cols, in0=cols, in1=k_sq_row[:, part(c, K_PASS)], op=ALU.subtract
+            )
+
         def clamp(g, cols, smallest):
             nc.vector.tensor_scalar(
                 out=scores[:, g, cols],
@@ -240,6 +247,7 @@ def tile_attention_pa_kernel(tc, q, k, x, Wv, out):
 
         every_key = slice(0, TOKENS)
         late = ((q_rows, q_mx, 1), (w_rows, w_mx, 0), (x_rows, x_mx, 0), (x_rows, x_mx, 1))
+        beside = (6, 7)
         qk_of = {0: products(0), 1: products(1)}
         subtract(0, 0, qk_of[0][0])
         subtract(0, 1, qk_of[0][1])
@@ -250,7 +258,7 @@ def tile_attention_pa_kernel(tc, q, k, x, Wv, out):
             if g < len(late):
                 rows, operand, c = late[g]
                 features_to_partitions(rows, operand, c, BOTH, nc.scalar.copy)
-            else:
+            elif g < len(late) + 2:
                 value_columns(0, g - len(late), nc.scalar.copy)
             if g + 2 < TILES:
                 qk_of[g + 2] = products(g + 2)
@@ -258,8 +266,10 @@ def tile_attention_pa_kernel(tc, q, k, x, Wv, out):
                 subtract(g + 1, 0, qk_of[g + 1][0])
             if g + 1 < TILES:
                 clamp(g, every_key, TOKENS)
-            if g + 1 < TILES:
+            if g + 1 < TILES and g + 1 not in beside:
                 subtract(g + 1, 1, qk_of[g + 1][1])
+            if g + 2 in beside:
+                subtract_beside(g + 2, 1, qk_of[g + 2][1])
             if g < len(late) - 1:
                 quantise(nc, operand, part(c, K_PASS))
             if g + 1 < TILES:
@@ -287,9 +297,12 @@ def tile_attention_pa_kernel(tc, q, k, x, Wv, out):
         )
 
         quantise(nc, x_mx, part(1, K_PASS))
-        quantise(nc, v_mx, part(0, FEATS))
+        for r in range(2, PACK):
+            value_columns(0, r, nc.vector.tensor_copy)
         for r in range(PACK):
             value_columns(1, r, nc.vector.tensor_copy)
+            if r == 0:
+                quantise(nc, v_mx, part(0, FEATS))
         spin(2)
         quantise(nc, v_mx, part(1, FEATS))
 

@@ -77,7 +77,7 @@ def tile_attention_pa_kernel(tc, q, k, x, Wv, out):
         quantised = ctx.enter_context(tc.tile_pool(name="quantised", bufs=5))
         psum = ctx.enter_context(tc.psum_pool(name="psum", bufs=4))
 
-        k_rows = load_tokens(nc, keep, k, "k_rows", (2, 2))
+        k_rows = load_tokens(nc, keep, k, "k_rows", (1, 2))
         q_rows = load_tokens(nc, keep, q, "q_rows", (2, PACK))
         w_rows = keep.tile([P, 1, FEATS // P, FEATS], BF16, name="w_rows")
         nc.sync.dma_start(out=w_rows[:, 0], in_=Wv.rearrange("(r p) f -> p r f", p=P))

from contextlib import ExitStack

import concourse.mybir as mybir
from concourse.masks import make_identity

F32 = mybir.dt.float32
BF16 = mybir.dt.bfloat16
U32 = mybir.dt.uint32
U8 = mybir.dt.uint8
FP8X4 = mybir.dt.float8_e4m3fn_x4
ALU = mybir.AluOpType
ACT = mybir.ActivationFunctionType

P = 128
PACK = 4
K_PASS = P * PACK
TOKENS = 1024
FEATS = 512
TILES = TOKENS // P
CHUNKS = TOKENS // K_PASS
BOTH = (0, 1)
HALVES = FEATS // 2 // P
ROW = TOKENS + 8

FLOPS = 2 * TOKENS * FEATS * FEATS + 2 * 2 * TOKENS * TOKENS * FEATS


def part(index, size):
    return slice(index * size, (index + 1) * size)


def load_tokens(nc, pool, src, name, tiles_a_load):
    rows = pool.tile([P, CHUNKS, PACK, FEATS], BF16, name=name)
    view = src.flatten_outer_dims().rearrange("(c p t) f -> p c t f", p=P, t=PACK)
    for c in range(CHUNKS):
        for i in range(PACK // tiles_a_load[c]):
            tiles = part(i, tiles_a_load[c])
            nc.sync.dma_start(out=rows[:, c, tiles], in_=view[:, c, tiles])
    return rows


def mx_tiles(pool, width, name):
    grouped = pool.tile([P, width, PACK], BF16, name=name + "_grouped", align_bytes=64)
    codes = pool.tile([P, width], U32, name=name + "_codes", align_bytes=64)
    scales = pool.tile([P, width], U8, name=name + "_scales", align_bytes=64)
    return grouped, codes, scales


def quantise(nc, operand, cols):
    grouped, codes, scales = operand
    nc.vector.quantize_mx(
        out=codes[:, cols].bitcast(FP8X4),
        scales=scales[:, cols],
        in_=grouped[:, cols, :].rearrange("p m t -> p (m t)"),
    )


def multiply(nc, acc, stationary, s_cols, moving, m_cols, start, stop):
    nc.tensor.matmul_mx(
        out=acc,
        lhsT=stationary[1][:, s_cols].bitcast(FP8X4),
        lhsT_scale=stationary[2][:, s_cols],
        rhs=moving[1][:, m_cols].bitcast(FP8X4),
        rhs_scale=moving[2][:, m_cols],
        start=start,
        stop=stop,
    )


def tile_attention_pa_kernel(tc, q, k, x, Wv, out):
    nc = tc.nc
    with ExitStack() as ctx:
        ctx.enter_context(tc.manual_schedule())
        keep = ctx.enter_context(tc.tile_pool(name="keep", bufs=1))
        work = ctx.enter_context(tc.tile_pool(name="work", bufs=3))
        results = ctx.enter_context(tc.tile_pool(name="results", bufs=TILES))
        quantised = ctx.enter_context(tc.tile_pool(name="quantised", bufs=5))
        psum = ctx.enter_context(tc.psum_pool(name="psum", bufs=4))

        k_rows = load_tokens(nc, keep, k, "k_rows", (1, 2))
        q_rows = load_tokens(nc, keep, q, "q_rows", (2, PACK))
        w_rows = keep.tile([P, 1, FEATS // P, FEATS], BF16, name="w_rows")
        nc.sync.dma_start(out=w_rows[:, 0], in_=Wv.rearrange("(r p) f -> p r f", p=P))
        x_rows = load_tokens(nc, keep, x, "x_rows", (PACK, PACK))

        ident_f32 = keep.tile([P, P], F32, name="ident_f32")
        make_identity(nc, ident_f32[:])

        zeros = keep.tile([P, FEATS], BF16, name="zeros")
        nc.gpsimd.memset(zeros[:], 0.0)

        def spin(passes):
            bank = psum.tile([P, FEATS], F32, tag="mm")
            for i in range(passes):
                nc.tensor.matmul(bank[:], lhsT=zeros[:, 0:P], rhs=zeros[:], start=True, stop=True)

        one = keep.tile([P, 1], F32, name="one")
        nc.vector.memset(one[:], 1.0)
        warm = keep.tile([P, 1], F32, name="warm")
        nc.scalar.activation(out=warm[:], in_=one[:], func=ACT.Sqrt)

        k_mx = mx_tiles(keep, TOKENS, "k")
        q_mx = mx_tiles(keep, TOKENS, "q")
        x_mx = mx_tiles(keep, TOKENS, "x")
        w_mx = mx_tiles(keep, FEATS, "w")
        v_mx = mx_tiles(keep, CHUNKS * FEATS, "v")

        k_sq = keep.tile([P, TILES], F32, name="k_sq")
        q_sq = keep.tile([P, TILES], F32, name="q_sq")
        q_sq_scaled = keep.tile([P, TILES], F32, name="q_sq_scaled")
        k_sq_row = keep.tile([P, TOKENS], F32, name="k_sq_row")
        scores = keep.tile([P, TILES, ROW], F32, name="scores")
        neg_max = keep.tile([P, TILES], F32, name="neg_max")
        row_sum = keep.tile([P, TILES], F32, name="row_sum")
        row_inv = keep.tile([P, TILES], F32, name="row_inv")
        out_view = out.flatten_outer_dims().rearrange("(c p t) d -> p c t d", p=P, t=PACK)

        def sum_of_squares(rows, sums, g):
            squares = work.tile([P, FEATS], BF16, tag="squares")
            nc.scalar.activation(
                out=squares[:],
                in_=rows[:, g // PACK, g % PACK, :],
                func=ACT.Square,
                accum_out=sums[:, g : g + 1],
            )

        def features_to_partitions(rows, operand, c, pairs, copy, interleave=False):
            words = rows[:].bitcast(F32)
            grouped_words = operand[0][:].bitcast(F32)
            for pair in pairs:
                bank = psum.tile([P, HALVES, 2 * P], F32, tag="tp")
                for a in range(2):
                    for u in range(HALVES):
                        nc.tensor.transpose(
                            bank[:, u, part(a, P)], words[:, c, 2 * pair + a, part(u, P)], ident_f32[:]
                        )
                cols = grouped_words[:, part(2 * c + pair, 2 * P), :]
                if interleave:
                    copy(
                        out=cols.rearrange("p (m a) u -> p m a u", a=2),
                        in_=bank[:].rearrange("p u (a m) -> p m a u", a=2),
                    )
                else:
                    copy(out=cols, in_=bank[:].rearrange("p u m -> p m u"))

        def spread_key_squares(c):
            bank = psum.tile([P, PACK, P], F32, tag="tp")
            for t in range(PACK):
                g = c * PACK + t
                nc.tensor.transpose(
                    bank[:, t, :], k_sq[:, g : g + 1].to_broadcast([P, P]), ident_f32[:]
                )
            return bank[:].rearrange("p (u e) m -> p u m e", e=2)

        def query_squares(g):
            sum_of_squares(q_rows, q_sq, g)
            nc.gpsimd.tensor_scalar(
                out=q_sq_scaled[:, g : g + 1],
                in0=q_sq[:, g : g + 1],
                scalar1=1.0 / FEATS,
                scalar2=0.0,
                op0=ALU.mult,
                op1=ALU.add,
            )

        for g in range(2):
            row = k_rows[:, 0, g, :]
            squares = work.tile([P, FEATS], BF16, tag="first_squares")
            nc.vector.scalar_tensor_tensor(
                out=squares[:],
                in0=row,
                scalar=1.0,
                in1=row,
                op0=ALU.mult,
                op1=ALU.mult,
                accum_out=k_sq[:, g : g + 1],
            )
        for g in range(2, TILES):
            sum_of_squares(k_rows, k_sq, g)
        features_to_partitions(k_rows, k_mx, 0, BOTH, nc.vector.tensor_copy, True)
        features_to_partitions(k_rows, k_mx, 1, (0,), nc.vector.tensor_copy, True)
        features_to_partitions(k_rows, k_mx, 1, (1,), nc.scalar.copy, True)
        quantise(nc, k_mx, part(0, K_PASS))
        features_to_partitions(q_rows, q_mx, 0, (0,), nc.vector.tensor_copy)
        row_view = k_sq_row[:].rearrange("p (c u m e) -> p c u m e", c=CHUNKS, u=2, e=2)
        nc.vector.tensor_copy(out=row_view[:, 0], in_=spread_key_squares(0))
        nc.scalar.copy(out=row_view[:, 1], in_=spread_key_squares(1))
        quantise(nc, q_mx, part(0, 2 * P))
        quantise(nc, k_mx, part(1, K_PASS))
        query_squares(0)
        features_to_partitions(q_rows, q_mx, 0, (1,), nc.scalar.copy)
        query_squares(1)
        query_squares(2)

        def products(g):
            banks = []
            for c in range(CHUNKS):
                qk = psum.tile([P, K_PASS], F32, tag="mm")
                multiply(nc, qk[:], q_mx, part(g, P), k_mx, part(c, K_PASS), True, True)
                banks.append(qk)
            return banks

        def subtract(g, c, bank):
            nc.vector.scalar_tensor_tensor(
                out=scores[:, g, part(c, K_PASS)],
                in0=bank[:],
                scalar=2.0,
                in1=k_sq_row[:, part(c, K_PASS)],
                op0=ALU.mult,
                op1=ALU.subtract,
            )

        def subtract_beside(g, c, bank):
            cols = scores[:, g, part(c, K_PASS)]
            nc.scalar.activation(out=cols, in_=bank[:], func=ACT.Copy, scale=2.0)
            nc.gpsimd.tensor_tensor(
                out=cols, in0=cols, in1=k_sq_row[:, part(c, K_PASS)], op=ALU.subtract
            )

        def clamp(g, cols, smallest):
            nc.vector.tensor_scalar(
                out=scores[:, g, cols],
                in0=scores[:, g, cols],
                scalar1=q_sq[:, g : g + 1],
                scalar2=None,
                op0=ALU.min,
                op1=ALU.min,
                accum_out=scores[:, g, smallest : smallest + 1],
            )

        def roots(g, cols):
            nc.scalar.activation(
                out=scores[:, g, cols],
                in_=scores[:, g, cols],
                func=ACT.Sqrt,
                bias=q_sq_scaled[:, g : g + 1],
                scale=-1.0 / FEATS,
            )

        def value_columns(c, r, copy):
            bank = psum.tile([P, PACK, P], F32, tag="tp")
            for t in range(PACK):
                multiply(nc, bank[:, t, :], x_mx, part(c * PACK + t, P), w_mx, part(r, P), True, True)
            copy(
                out=v_mx[0][:, part(c * PACK + r, P), :], in_=bank[:].rearrange("p t d -> p d t")
            )

        every_key = slice(0, TOKENS)
        late = ((q_rows, q_mx, 1), (w_rows, w_mx, 0), (x_rows, x_mx, 0), (x_rows, x_mx, 1))
        beside = (6, 7)
        qk_of = {0: products(0), 1: products(1)}
        subtract(0, 0, qk_of[0][0])
        subtract(0, 1, qk_of[0][1])
        quantise(nc, q_mx, part(1, 2 * P))
        for g in range(TILES):
            if g + 3 < TILES:
                query_squares(g + 3)
            if g < len(late):
                rows, operand, c = late[g]
                features_to_partitions(rows, operand, c, BOTH, nc.scalar.copy)
            elif g < len(late) + 2:
                value_columns(0, g - len(late), nc.scalar.copy)
            if g + 2 < TILES:
                qk_of[g + 2] = products(g + 2)
            if g + 1 < TILES:
                subtract(g + 1, 0, qk_of[g + 1][0])
            if g + 1 < TILES:
                clamp(g, every_key, TOKENS)
            if g + 1 < TILES and g + 1 not in beside:
                subtract(g + 1, 1, qk_of[g + 1][1])
            if g + 2 in beside:
                subtract_beside(g + 2, 1, qk_of[g + 2][1])
            if g < len(late) - 1:
                quantise(nc, operand, part(c, K_PASS))
            if g + 1 < TILES:
                roots(g, slice(0, TOKENS + 1))
                nc.gpsimd.tensor_scalar(
                    out=neg_max[:, g : g + 1],
                    in0=scores[:, g, TOKENS : TOKENS + 1],
                    scalar1=-1.0,
                    scalar2=0.0,
                    op0=ALU.mult,
                    op1=ALU.add,
                )
        last = TILES - 1
        clamp(last, part(0, K_PASS), TOKENS)
        clamp(last, part(1, K_PASS), TOKENS + 1)
        roots(last, part(0, K_PASS))
        roots(last, slice(K_PASS, TOKENS + 2))
        nc.gpsimd.tensor_scalar(
            out=neg_max[:, last : last + 1],
            in0=scores[:, last, TOKENS : TOKENS + 1],
            scalar1=scores[:, last, TOKENS + 1 : TOKENS + 2],
            scalar2=-1.0,
            op0=ALU.max,
            op1=ALU.mult,
        )

        quantise(nc, x_mx, part(1, K_PASS))
        for r in range(2, PACK):
            value_columns(0, r, nc.vector.tensor_copy)
        for r in range(PACK):
            value_columns(1, r, nc.vector.tensor_copy)
            if r == 0:
                quantise(nc, v_mx, part(0, FEATS))
        spin(2)
        quantise(nc, v_mx, part(1, FEATS))

        def exps(g, e_rows, cols, sums):
            nc.scalar.activation(
                out=e_rows[:, cols],
                in_=scores[:, g, cols],
                func=ACT.Exp,
                bias=neg_max[:, g : g + 1],
                scale=1.0,
                accum_out=sums,
            )

        def keys_to_partitions(e_rows, e_grouped, chunks):
            words = e_rows[:].bitcast(F32)
            bank = psum.tile([P, len(chunks), 2, P], F32, tag="tp")
            for i, c in enumerate(chunks):
                for u in range(2):
                    nc.tensor.transpose(bank[:, i, u, :], words[:, part(2 * c + u, P)], ident_f32[:])
            grouped_words = e_grouped[:].bitcast(F32).rearrange("p (c i) u -> p c i u", c=CHUNKS)
            nc.vector.tensor_copy(
                out=grouped_words[:, chunks[0] : chunks[-1] + 1],
                in_=bank[:].rearrange("p c u i -> p c i u"),
            )

        def invert_sums(tiles):
            nc.vector.reciprocal(out=row_inv[:, tiles], in_=row_sum[:, tiles])

        def weight_tiles():
            e_rows = work.tile([P, TOKENS], BF16, tag="e_rows")
            e_grouped = work.tile([P, CHUNKS * P, PACK], BF16, tag="e_grouped", align_bytes=64)
            e_codes = quantised.tile([P, CHUNKS * P], U32, tag="e_codes", align_bytes=64)
            e_scales = quantised.tile([P, CHUNKS * P], U8, tag="e_scales", align_bytes=64)
            return e_rows, (e_grouped, e_codes, e_scales)

        def weighted_sum(e_mx, cols):
            acc = psum.tile([P, cols.stop - cols.start], F32, tag="mm")
            for c in range(CHUNKS):
                v_cols = slice(c * FEATS + cols.start, c * FEATS + cols.stop)
                multiply(nc, acc[:], e_mx, part(c, P), v_mx, v_cols, c == 0, c == CHUNKS - 1)
            return acc

        def finish(g, cols, acc, on_scalar):
            result = results.tile([P, cols.stop - cols.start], F32, tag="result")
            inverse = row_inv[:, g : g + 1]
            if on_scalar:
                nc.scalar.activation(out=result[:], in_=acc[:], func=ACT.Copy, scale=inverse)
            else:
                nc.vector.tensor_scalar_mul(out=result[:], in0=acc[:], scalar1=inverse)
            nc.sync.dma_start(out=out_view[:, g // PACK, g % PACK, cols], in_=result[:])

        every = slice(0, FEATS)
        e_of = {}
        acc_of = {}
        for g in range(last):
            e_rows, e_of[g] = weight_tiles()
            exps(g, e_rows, slice(0, TOKENS), row_sum[:, g : g + 1])
            keys_to_partitions(e_rows, e_of[g][0], BOTH)
            if g >= 3:
                acc_of[g - 3] = weighted_sum(e_of[g - 3], every)
            else:
                spin(2)
            if g >= 1:
                quantise(nc, e_of[g - 1], part(0, CHUNKS * P))
            if g in (2, 4, 6):
                invert_sums(slice(g - 2, g))
            if g in (4, 5):
                finish(g - 4, every, acc_of[g - 4], False)
        e_rows, e_of[last] = weight_tiles()
        halves = keep.tile([P, CHUNKS], F32, name="halves")
        for c in range(CHUNKS):
            exps(last, e_rows, part(c, K_PASS), halves[:, c : c + 1])
            keys_to_partitions(e_rows, e_of[last][0], (c,))
            if c == 0:
                acc_of[4] = weighted_sum(e_of[4], every)
                quantise(nc, e_of[last - 1], part(0, CHUNKS * P))
        acc_of[5] = weighted_sum(e_of[5], every)
        nc.vector.tensor_add(out=row_sum[:, last:], in0=halves[:, 0:1], in1=halves[:, 1:2])
        quantise(nc, e_of[last], part(0, P))
        quantise(nc, e_of[last], part(1, P))
        invert_sums(slice(last - 1, TILES))
        finish(2, every, acc_of[2], True)
        acc_of[last - 1] = weighted_sum(e_of[last - 1], every)
        finish(3, every, acc_of[3], True)
        left = weighted_sum(e_of[last], part(0, FEATS // 2))
        finish(4, every, acc_of[4], True)
        right = weighted_sum(e_of[last], part(1, FEATS // 2))
        finish(5, every, acc_of[5], True)
        finish(6, every, acc_of[6], False)
        finish(last, part(0, FEATS // 2), left, False)
        finish(last, part(1, FEATS // 2), right, True)
